import numpy as np
import ml_dtypes


def mxq(x, axis, fmt="e4m3"):
    dtype, down = {"e4m3": (ml_dtypes.float8_e4m3fn, 7), "e5m2": (ml_dtypes.float8_e5m2, 14)}[fmt]
    v = np.moveaxis(np.asarray(x, np.float32).astype(ml_dtypes.bfloat16).astype(np.float64), axis, -1)
    blocks = v.reshape(v.shape[:-1] + (-1, 32))
    amax = np.abs(blocks).max(-1, keepdims=True)
    byte = np.maximum(np.where(amax > 0, np.frexp(amax)[1] - 1 + 127, 0) - down, 1)
    scale = np.exp2(byte - 127.0)
    codes = (blocks / scale).astype(np.float32).astype(dtype).astype(np.float64)
    return np.moveaxis((codes * scale).reshape(v.shape), -1, axis)


WIDE = False


def mx_kscale(k):
    if not WIDE:
        return np.ones(k)
    levels = np.array([10, -10, 5, -5, 0])
    if k % 512:
        return np.exp2(np.random.permutation(np.resize(levels, k // 32))).repeat(32)
    a = np.empty((k // 512, 16))
    for p in range(k // 512):
        a[p, :8] = np.random.permutation(np.resize(levels, 8))
        for g in range(8):
            far = levels[np.abs(levels - a[p, g]) >= 10]
            a[p, g + 8] = far[np.random.randint(len(far))]
    return np.exp2(a.ravel()).repeat(32)


BF16 = ml_dtypes.bfloat16


def bf(x):
    return np.asarray(x, np.float32).astype(BF16)


def f64(x):
    return np.asarray(x).astype(np.float64)


B, S, D, H, HD, FF = 4, 2048, 512, 1, 128, 8192
EPS = 1e-05


def layer_norm(x, scale, bias):
    mu = x.mean(-1, keepdims=True)
    var = x.var(-1, keepdims=True)
    return (x - mu) / np.sqrt(var + EPS) * scale + bias


def setup_inputs():
    s = mx_kscale(D)
    return {
        "x": bf(np.random.standard_normal((B, S, D)) + 0.5 * np.random.standard_normal((B, S, 1))),
        "ln1_s": bf((1.0 + 0.1 * np.random.standard_normal(D)) * s),
        "ln1_b": bf(0.1 * np.random.standard_normal(D) * s),
        "wq_k": bf(np.random.standard_normal((D, H, HD)) / np.sqrt(D) / s[:, None, None]),
        "wq_b": bf(0.1 * np.random.standard_normal((H, HD))),
        "wk_k": bf(np.random.standard_normal((D, HD)) / np.sqrt(D) / s[:, None]),
        "wk_b": bf(0.1 * np.random.standard_normal(HD)),
        "wv_k": bf(np.random.standard_normal((D, HD)) / np.sqrt(D) / s[:, None]),
        "wv_b": bf(0.1 * np.random.standard_normal(HD)),
    }


def reference(x, ln1_s, ln1_b, wq_k, wq_b, wk_k, wk_b, wv_k, wv_b):
    h = layer_norm(f64(x), f64(ln1_s), f64(ln1_b))
    hq = mxq(h, 2, "e4m3")
    q = (hq @ mxq(f64(wq_k).reshape(D, H * HD), 0, "e4m3")).reshape(B, S, H, HD) + f64(wq_b)
    k = (hq @ mxq(f64(wk_k), 0, "e4m3")) + f64(wk_b)
    v = (hq @ mxq(f64(wv_k), 0, "e4m3")) + f64(wv_b)
    return q, k, v

@@ -1,0 +1,223 @@
+from contextlib import ExitStack
+
+import concourse.mybir as mybir
+from concourse.masks import make_identity
+
+F32 = mybir.dt.float32
+BF16 = mybir.dt.bfloat16
+U32 = mybir.dt.uint32
+U8 = mybir.dt.uint8
+FP8X4 = mybir.dt.float8_e4m3fn_x4
+ALU = mybir.AluOpType
+ACT = mybir.ActivationFunctionType
+
+P = 128
+D = 512
+PACK = 4
+E = 128
+NPROJ = 3
+TOKENS = 4 * 2048
+GT = 4
+GTOK = GT * P
+NG = TOKENS // GTOK
+EPS = 1e-05
+TRB = 5
+
+FLOPS = 2 * TOKENS * D * NPROJ * E
+
+
+def tile_transformerlayer_pa_t_kernel(
+    tc, x, ln1_s, ln1_b, wq_k, wq_b, wk_k, wk_b, wv_k, wv_b, out_0, out_1, out_2
+):
+    nc = tc.nc
+    xg = x.rearrange("b s d -> (b s) d").rearrange("(g p j) d -> g p (j d)", p=P, j=GT)
+    outs = [
+        out_0.rearrange("b s h e -> (b s h) e").rearrange("(g p j) e -> g p (j e)", p=P, j=GT),
+        out_1.rearrange("b s e -> (b s) e").rearrange("(g p j) e -> g p (j e)", p=P, j=GT),
+        out_2.rearrange("b s e -> (b s) e").rearrange("(g p j) e -> g p (j e)", p=P, j=GT),
+    ]
+
+    with ExitStack() as ctx:
+        const = ctx.enter_context(tc.tile_pool(name="const", bufs=1))
+        xpool = ctx.enter_context(tc.tile_pool(name="xpool", bufs=NG))
+        small = ctx.enter_context(tc.tile_pool(name="small", bufs=4))
+        zpool = ctx.enter_context(tc.tile_pool(name="zpool", bufs=3))
+        hpool = ctx.enter_context(tc.tile_pool(name="hpool", bufs=3))
+        qpool = ctx.enter_context(tc.tile_pool(name="qpool", bufs=3))
+        opool = ctx.enter_context(tc.tile_pool(name="opool", bufs=4))
+        psum = ctx.enter_context(tc.psum_pool(name="psum", bufs=1))
+        ctx.enter_context(tc.manual_schedule())
+
+        xt = []
+        for g in range(NG):
+            x_t = xpool.tile([P, GT, D], BF16, name="x_t")
+            nc.sync.dma_start(out=x_t[:].rearrange("p j d -> p (j d)"), in_=xg[g])
+            xt.append(x_t)
+
+        sraw = const.tile([P, PACK], BF16, name="sraw")
+        braw = const.tile([P, PACK], BF16, name="braw")
+        eps_t = const.tile([P, 1], F32, name="eps_t")
+        nc.vector.memset(eps_t[:], EPS)
+        nc.scalar.dma_start(out=sraw[:], in_=ln1_s.rearrange("(p t) -> p t", t=PACK))
+        nc.scalar.dma_start(out=braw[:], in_=ln1_b.rearrange("(p t) -> p t", t=PACK))
+        wraw = const.tile([P, PACK, NPROJ * E], BF16, name="wraw")
+        nc.scalar.dma_start(out=wraw[:, :, 0:E], in_=wq_k.rearrange("(p t) h e -> p t (h e)", t=PACK))
+        nc.scalar.dma_start(out=wraw[:, :, E : 2 * E], in_=wk_k.rearrange("(p t) e -> p t e", t=PACK))
+        nc.scalar.dma_start(out=wraw[:, :, 2 * E : 3 * E], in_=wv_k.rearrange("(p t) e -> p t e", t=PACK))
+
+        ident = const.tile([P, P], F32, name="ident")
+        make_identity(nc, ident[:])
+        bias = const.tile([P, NPROJ, E], BF16, name="bias")
+        nc.gpsimd.dma_start(out=bias[:, 0, :], in_=wq_b.rearrange("h e -> (h e)").partition_broadcast(P))
+        nc.gpsimd.dma_start(out=bias[:, 1, :], in_=wk_b.partition_broadcast(P))
+        nc.gpsimd.dma_start(out=bias[:, 2, :], in_=wv_b.partition_broadcast(P))
+
+        sbcol = const.tile([P, 2 * PACK], F32, name="sbcol")
+        wcodes = const.tile([P, NPROJ * E], U32, name="wcodes", align_bytes=64)
+        wscl = const.tile([P, NPROJ * E], U8, name="wscl", align_bytes=64)
+
+        def setup_a():
+            nc.vector.tensor_copy(out=sbcol[:, 0:PACK], in_=sraw[:])
+            nc.vector.tensor_copy(out=sbcol[:, PACK : 2 * PACK], in_=braw[:])
+
+        def setup_b():
+            wgrp = const.tile([P, NPROJ * E, PACK], BF16, name="wgrp", align_bytes=64)
+            nc.vector.tensor_copy(out=wgrp[:], in_=wraw[:].rearrange("p t n -> p n t"))
+            for pr in range(NPROJ):
+                cols = slice(pr * E, (pr + 1) * E)
+                nc.vector.quantize_mx(
+                    out=wcodes[:, cols].bitcast(FP8X4),
+                    scales=wscl[:, cols],
+                    in_=wgrp[:, cols, :].rearrange("p n t -> p (n t)"),
+                )
+
+        S = {}
+
+        def stats(g):
+            st = small.tile([P, GT, 6], F32, name="st")
+            mv = small.tile([P, GT, 2], F32, name="mv")
+            for j in range(GT):
+                nc.vector.bn_stats(out=st[:, j, :], in_=xt[g][:, j, :])
+            for j in range(GT):
+                nc.vector.bn_aggr(out=mv[:, j, :], in_=st[:, j, :])
+            S[("mv", g)] = mv
+
+        def rstd_of(g):
+            mv = S[("mv", g)]
+            sd = small.tile([P, GT], F32, name="sd")
+            nc.scalar.activation(out=sd[:], in_=mv[:, :, 1], func=ACT.Sqrt, bias=eps_t[:, 0:1], scale=1.0)
+            rstd = small.tile([P, GT], F32, name="rstd")
+            nc.vector.reciprocal(out=rstd[:], in_=sd[:])
+            negmu = small.tile([P, GT], F32, name="negmu")
+            nc.vector.tensor_scalar_mul(out=negmu[:], in0=mv[:, :, 0], scalar1=-1.0)
+            S[("rs", g)] = (rstd, negmu)
+
+        def normalise(g):
+            rstd, negmu = S[("rs", g)]
+            z = zpool.tile([P, GT, D], F32, name="z")
+            for j in range(GT):
+                nc.gpsimd.tensor_scalar(
+                    out=z[:, j, :],
+                    in0=xt[g][:, j, :],
+                    scalar1=negmu[:, j : j + 1],
+                    scalar2=rstd[:, j : j + 1],
+                    op0=ALU.add,
+                    op1=ALU.mult,
+                )
+            S[("z", g)] = z
+
+        def transposes(g):
+            z = S[("z", g)]
+            banks = []
+            for t in range(PACK):
+                bank = psum.tile([P, GTOK], F32, name="trb", tag="tr%d" % ((PACK * g + t) % TRB))
+                for j in range(GT):
+                    nc.tensor.transpose(bank[:, j * P : (j + 1) * P], z[:, j, t::PACK], ident[:])
+                banks.append(bank)
+            S[("tr", g)] = banks
+
+        def affine(g):
+            banks = S[("tr", g)]
+            hT = hpool.tile([P, PACK, GTOK], BF16, name="hT")
+            for t in range(PACK):
+                nc.scalar.activation(
+                    out=hT[:, t, :],
+                    in_=banks[t][:],
+                    func=ACT.Identity,
+                    scale=sbcol[:, t : t + 1],
+                    bias=sbcol[:, PACK + t : PACK + t + 1],
+                )
+            S[("hT", g)] = hT
+
+        def regroup(g):
+            hT = S[("hT", g)]
+            hG = hpool.tile([P, GTOK, PACK], BF16, name="hG", align_bytes=64)
+            nc.scalar.copy(
+                out=hG[:].rearrange("p (c i) t -> p c t i", i=4),
+                in_=hT[:].rearrange("p t (c i) -> p c t i", i=4),
+            )
+            S[("hG", g)] = hG
+
+        def quantise(g):
+            hG = S[("hG", g)]
+            codes = qpool.tile([P, GTOK], U32, name="codes", align_bytes=64)
+            scl = qpool.tile([P, GTOK], U8, name="scl", align_bytes=64)
+            nc.vector.quantize_mx(
+                out=codes[:].bitcast(FP8X4), scales=scl[:], in_=hG[:].rearrange("p c t -> p (c t)")
+            )
+            S[("q", g)] = (codes, scl)
+
+        def project(g):
+            codes, scl = S[("q", g)]
+            banks = []
+            for pr in range(NPROJ):
+                bank = psum.tile([P, GT * E], F32, name="mmb", tag="mm%d" % pr)
+                wc = slice(pr * E, (pr + 1) * E)
+                for j in range(GT):
+                    tk = slice(j * P, (j + 1) * P)
+                    nc.tensor.matmul_mx(
+                        out=bank[:, j * E : (j + 1) * E],
+                        lhsT=codes[:, tk].bitcast(FP8X4),
+                        lhsT_scale=scl[:, tk],
+                        rhs=wcodes[:, wc].bitcast(FP8X4),
+                        rhs_scale=wscl[:, wc],
+                        start=True,
+                        stop=True,
+                    )
+                banks.append(bank)
+            S[("mm", g)] = banks
+
+        def finish(g):
+            banks = S[("mm", g)]
+            o = opool.tile([P, NPROJ, GT * E], F32, name="o")
+            for pr in range(NPROJ):
+                nc.vector.tensor_tensor(
+                    out=o[:, pr, :].rearrange("p (j e) -> p j e", e=E),
+                    in0=banks[pr][:].rearrange("p (j e) -> p j e", e=E),
+                    in1=bias[:, pr, :].unsqueeze(1).to_broadcast([P, GT, E]),
+                    op=ALU.add,
+                )
+                nc.sync.dma_start(out=outs[pr][g], in_=o[:, pr, :])
+
+        for i in range(NG + 5):
+            if 0 <= i - 1 < NG:
+                rstd_of(i - 1)
+                normalise(i - 1)
+            if 0 <= i - 2 < NG:
+                affine(i - 2)
+            if 0 <= i - 1 < NG:
+                transposes(i - 1)
+            if 0 <= i - 2 < NG:
+                regroup(i - 2)
+            if i < NG:
+                stats(i)
+            if i == 0:
+                setup_a()
+            if i == 1:
+                setup_b()
+            if 0 <= i - 3 < NG:
+                quantise(i - 3)
+            if 0 <= i - 4 < NG:
+                finish(i - 4)
+            if 0 <= i - 3 < NG:
+                project(i - 3)

@@ -21,7 +21,8 @@ GT = 4
 GTOK = GT * P
 NG = TOKENS // GTOK
 EPS = 1e-05
-TRB = 5
+TRB = 4
+V_REGROUP = (12, 14)
 
 FLOPS = 2 * TOKENS * D * NPROJ * E
 
@@ -40,8 +41,8 @@ def tile_transformerlayer_pa_t_kernel(
     with ExitStack() as ctx:
         const = ctx.enter_context(tc.tile_pool(name="const", bufs=1))
         xpool = ctx.enter_context(tc.tile_pool(name="xpool", bufs=NG))
-        small = ctx.enter_context(tc.tile_pool(name="small", bufs=4))
-        zpool = ctx.enter_context(tc.tile_pool(name="zpool", bufs=3))
+        small = ctx.enter_context(tc.tile_pool(name="small", bufs=8))
+        zpool = ctx.enter_context(tc.tile_pool(name="zpool", bufs=4))
         hpool = ctx.enter_context(tc.tile_pool(name="hpool", bufs=3))
         qpool = ctx.enter_context(tc.tile_pool(name="qpool", bufs=3))
         opool = ctx.enter_context(tc.tile_pool(name="opool", bufs=4))
@@ -51,38 +52,55 @@ def tile_transformerlayer_pa_t_kernel(
         xt = []
         for g in range(NG):
             x_t = xpool.tile([P, GT, D], BF16, name="x_t")
-            nc.sync.dma_start(out=x_t[:].rearrange("p j d -> p (j d)"), in_=xg[g])
             xt.append(x_t)
-
+        wraw = const.tile([P, PACK, NPROJ * E], BF16, name="wraw")
         sraw = const.tile([P, PACK], BF16, name="sraw")
         braw = const.tile([P, PACK], BF16, name="braw")
-        eps_t = const.tile([P, 1], F32, name="eps_t")
-        nc.vector.memset(eps_t[:], EPS)
-        nc.scalar.dma_start(out=sraw[:], in_=ln1_s.rearrange("(p t) -> p t", t=PACK))
-        nc.scalar.dma_start(out=braw[:], in_=ln1_b.rearrange("(p t) -> p t", t=PACK))
-        wraw = const.tile([P, PACK, NPROJ * E], BF16, name="wraw")
-        nc.scalar.dma_start(out=wraw[:, :, 0:E], in_=wq_k.rearrange("(p t) h e -> p t (h e)", t=PACK))
-        nc.scalar.dma_start(out=wraw[:, :, E : 2 * E], in_=wk_k.rearrange("(p t) e -> p t e", t=PACK))
-        nc.scalar.dma_start(out=wraw[:, :, 2 * E : 3 * E], in_=wv_k.rearrange("(p t) e -> p t e", t=PACK))
+        brow = const.tile([P, NPROJ * E], BF16, name="brow")
+        nc.vector.memset(brow[:], 0.0)
+
+        for j in range(GT):
+            nc.sync.dma_start(out=xt[0][:, j, :], in_=xg[0][:, j * D : (j + 1) * D])
+        nc.sync.dma_start(out=sraw[:], in_=ln1_s.rearrange("(p t) -> p t", t=PACK))
+        nc.sync.dma_start(out=braw[:], in_=ln1_b.rearrange("(p t) -> p t", t=PACK))
+        for g in (1, 2):
+            nc.sync.dma_start(out=xt[g][:].rearrange("p j d -> p (j d)"), in_=xg[g])
+        nc.sync.dma_start(out=wraw[:, :, 0:E], in_=wq_k.rearrange("(p t) h e -> p t (h e)", t=PACK))
+        nc.sync.dma_start(out=wraw[:, :, E : 2 * E], in_=wk_k.rearrange("(p t) e -> p t e", t=PACK))
+        nc.sync.dma_start(out=wraw[:, :, 2 * E : 3 * E], in_=wv_k.rearrange("(p t) e -> p t e", t=PACK))
+        nc.sync.dma_start(out=xt[3][:].rearrange("p j d -> p (j d)"), in_=xg[3])
+        nc.sync.dma_start(out=brow[0:1, 0:E], in_=wq_b)
+        nc.sync.dma_start(out=brow[0:1, E : 2 * E], in_=wk_b.unsqueeze(0))
+        nc.sync.dma_start(out=brow[0:1, 2 * E : 3 * E], in_=wv_b.unsqueeze(0))
+        for g in range(4, NG):
+            nc.sync.dma_start(out=xt[g][:].rearrange("p j d -> p (j d)"), in_=xg[g])
 
         ident = const.tile([P, P], F32, name="ident")
         make_identity(nc, ident[:])
-        bias = const.tile([P, NPROJ, E], BF16, name="bias")
-        nc.gpsimd.dma_start(out=bias[:, 0, :], in_=wq_b.rearrange("h e -> (h e)").partition_broadcast(P))
-        nc.gpsimd.dma_start(out=bias[:, 1, :], in_=wk_b.partition_broadcast(P))
-        nc.gpsimd.dma_start(out=bias[:, 2, :], in_=wv_b.partition_broadcast(P))
+        eps_t = const.tile([P, 1], F32, name="eps_t")
+        zero_t = const.tile([P, 1], F32, name="zero_t")
+        nc.gpsimd.memset(zero_t[:], 0.0)
+        nc.gpsimd.tensor_scalar(
+            out=eps_t[:], in0=zero_t[:], scalar1=EPS, scalar2=1.0, op0=ALU.add, op1=ALU.mult
+        )
+        ones = const.tile([P, P], BF16, name="ones")
+        nc.gpsimd.memset(ones[:], 1.0)
 
-        sbcol = const.tile([P, 2 * PACK], F32, name="sbcol")
+        scol = const.tile([P, PACK], F32, name="scol")
+        bcol = const.tile([P, PACK], F32, name="bcol")
+        bias = const.tile([P, NPROJ * E], F32, name="bias")
         wcodes = const.tile([P, NPROJ * E], U32, name="wcodes", align_bytes=64)
         wscl = const.tile([P, NPROJ * E], U8, name="wscl", align_bytes=64)
+        wgrp = const.tile([P, NPROJ * E, PACK], BF16, name="wgrp", align_bytes=64)
 
-        def setup_a():
-            nc.vector.tensor_copy(out=sbcol[:, 0:PACK], in_=sraw[:])
-            nc.vector.tensor_copy(out=sbcol[:, PACK : 2 * PACK], in_=braw[:])
+        def setup_gain():
+            nc.vector.tensor_copy(out=scol[:], in_=sraw[:])
+            nc.vector.tensor_copy(out=bcol[:], in_=braw[:])
 
-        def setup_b():
-            wgrp = const.tile([P, NPROJ * E, PACK], BF16, name="wgrp", align_bytes=64)
-            nc.vector.tensor_copy(out=wgrp[:], in_=wraw[:].rearrange("p t n -> p n t"))
+        def setup_group_weights():
+            nc.scalar.copy(out=wgrp[:], in_=wraw[:].rearrange("p t n -> p n t"))
+
+        def setup_quantise_weights():
             for pr in range(NPROJ):
                 cols = slice(pr * E, (pr + 1) * E)
                 nc.vector.quantize_mx(
@@ -90,6 +108,11 @@ def tile_transformerlayer_pa_t_kernel(
                     scales=wscl[:, cols],
                     in_=wgrp[:, cols, :].rearrange("p n t -> p (n t)"),
                 )
+
+        def setup_bias():
+            ps = psum.tile([P, GT * E], F32, name="ps_bias", tag="mm0")
+            nc.tensor.matmul(ps[:, 0 : NPROJ * E], lhsT=ones[:], rhs=brow[:], start=True, stop=True)
+            nc.vector.tensor_copy(out=bias[:], in_=ps[:, 0 : NPROJ * E])
 
         S = {}
 
@@ -104,16 +127,16 @@ def tile_transformerlayer_pa_t_kernel(
 
         def rstd_of(g):
             mv = S[("mv", g)]
-            sd = small.tile([P, GT], F32, name="sd")
-            nc.scalar.activation(out=sd[:], in_=mv[:, :, 1], func=ACT.Sqrt, bias=eps_t[:, 0:1], scale=1.0)
-            rstd = small.tile([P, GT], F32, name="rstd")
-            nc.vector.reciprocal(out=rstd[:], in_=sd[:])
             negmu = small.tile([P, GT], F32, name="negmu")
-            nc.vector.tensor_scalar_mul(out=negmu[:], in0=mv[:, :, 0], scalar1=-1.0)
-            S[("rs", g)] = (rstd, negmu)
+            nc.scalar.activation(out=negmu[:], in_=mv[:, :, 0], func=ACT.Copy, scale=-1.0)
+            rstd = small.tile([P, GT], F32, name="rstd")
+            nc.scalar.activation(
+                out=rstd[:], in_=mv[:, :, 1], func=ACT.Abs_reciprocal_sqrt, bias=eps_t[:, 0:1], scale=1.0
+            )
+            S[("rs", g)] = (negmu, rstd)
 
         def normalise(g):
-            rstd, negmu = S[("rs", g)]
+            negmu, rstd = S[("rs", g)]
             z = zpool.tile([P, GT, D], F32, name="z")
             for j in range(GT):
                 nc.gpsimd.tensor_scalar(
@@ -144,18 +167,20 @@ def tile_transformerlayer_pa_t_kernel(
                     out=hT[:, t, :],
                     in_=banks[t][:],
                     func=ACT.Identity,
-                    scale=sbcol[:, t : t + 1],
-                    bias=sbcol[:, PACK + t : PACK + t + 1],
+                    scale=scol[:, t : t + 1],
+                    bias=bcol[:, t : t + 1],
                 )
             S[("hT", g)] = hT
 
         def regroup(g):
             hT = S[("hT", g)]
             hG = hpool.tile([P, GTOK, PACK], BF16, name="hG", align_bytes=64)
-            nc.scalar.copy(
-                out=hG[:].rearrange("p (c i) t -> p c t i", i=4),
-                in_=hT[:].rearrange("p t (c i) -> p c t i", i=4),
-            )
+            dst = hG[:].rearrange("p (c i) t -> p c t i", i=4)
+            src = hT[:].rearrange("p t (c i) -> p c t i", i=4)
+            if g in V_REGROUP:
+                nc.vector.tensor_copy(out=dst, in_=src)
+            else:
+                nc.scalar.copy(out=dst, in_=src)
             S[("hG", g)] = hG
 
         def quantise(g):
@@ -189,35 +214,38 @@ def tile_transformerlayer_pa_t_kernel(
 
         def finish(g):
             banks = S[("mm", g)]
-            o = opool.tile([P, NPROJ, GT * E], F32, name="o")
             for pr in range(NPROJ):
+                o = opool.tile([P, GT * E], F32, name="o%d" % pr)
                 nc.vector.tensor_tensor(
-                    out=o[:, pr, :].rearrange("p (j e) -> p j e", e=E),
+                    out=o[:].rearrange("p (j e) -> p j e", e=E),
                     in0=banks[pr][:].rearrange("p (j e) -> p j e", e=E),
-                    in1=bias[:, pr, :].unsqueeze(1).to_broadcast([P, GT, E]),
+                    in1=bias[:, pr * E : (pr + 1) * E].unsqueeze(1).to_broadcast([P, GT, E]),
                     op=ALU.add,
                 )
-                nc.sync.dma_start(out=outs[pr][g], in_=o[:, pr, :])
+                nc.sync.dma_start(out=outs[pr][g], in_=o[:])
 
-        for i in range(NG + 5):
-            if 0 <= i - 1 < NG:
-                rstd_of(i - 1)
-                normalise(i - 1)
-            if 0 <= i - 2 < NG:
-                affine(i - 2)
-            if 0 <= i - 1 < NG:
-                transposes(i - 1)
-            if 0 <= i - 2 < NG:
-                regroup(i - 2)
-            if i < NG:
-                stats(i)
-            if i == 0:
-                setup_a()
-            if i == 1:
-                setup_b()
-            if 0 <= i - 3 < NG:
-                quantise(i - 3)
-            if 0 <= i - 4 < NG:
-                finish(i - 4)
-            if 0 <= i - 3 < NG:
-                project(i - 3)
+        for n in range(-4, NG + 3):
+            if 0 <= n < NG:
+                affine(n)
+            if 0 <= n + 1 < NG:
+                transposes(n + 1)
+            if 0 <= n + 3 < NG:
+                rstd_of(n + 3)
+                normalise(n + 3)
+            if 0 <= n - 3 < NG:
+                finish(n - 3)
+            if 0 <= n - 1 < NG:
+                regroup(n - 1)
+            if 0 <= n - 2 < NG:
+                quantise(n - 2)
+            if n + 4 < NG:
+                stats(n + 4)
+            if n == -4:
+                setup_gain()
+            if n == -2:
+                setup_group_weights()
+            if n == -1:
+                setup_quantise_weights()
+                setup_bias()
+            if 0 <= n - 2 < NG:
+                project(n - 2)

@@ -88,7 +88,7 @@ def tile_transformerlayer_pa_t_kernel(
 
         scol = const.tile([P, PACK], F32, name="scol")
         bcol = const.tile([P, PACK], F32, name="bcol")
-        bias = const.tile([P, NPROJ * E], F32, name="bias")
+        bias = const.tile([P, NPROJ * E], BF16, name="bias")
         wcodes = const.tile([P, NPROJ * E], U32, name="wcodes", align_bytes=64)
         wscl = const.tile([P, NPROJ * E], U8, name="wscl", align_bytes=64)
         wgrp = const.tile([P, NPROJ * E, PACK], BF16, name="wgrp", align_bytes=64)
@@ -125,23 +125,23 @@ def tile_transformerlayer_pa_t_kernel(
                 nc.vector.bn_aggr(out=mv[:, j, :], in_=st[:, j, :])
             S[("mv", g)] = mv
 
-        def rstd_of(g):
+        def deviation(g):
             mv = S[("mv", g)]
             negmu = small.tile([P, GT], F32, name="negmu")
             nc.scalar.activation(out=negmu[:], in_=mv[:, :, 0], func=ACT.Copy, scale=-1.0)
-            rstd = small.tile([P, GT], F32, name="rstd")
-            nc.scalar.activation(
-                out=rstd[:], in_=mv[:, :, 1], func=ACT.Abs_reciprocal_sqrt, bias=eps_t[:, 0:1], scale=1.0
-            )
-            S[("rs", g)] = (negmu, rstd)
+            sd = small.tile([P, GT], F32, name="sd")
+            nc.scalar.activation(out=sd[:], in_=mv[:, :, 1], func=ACT.Sqrt, bias=eps_t[:, 0:1], scale=1.0)
+            S[("rs", g)] = (negmu, sd)
 
         def normalise(g):
-            negmu, rstd = S[("rs", g)]
-            z = zpool.tile([P, GT, D], F32, name="z")
+            negmu, sd = S[("rs", g)]
+            rstd = small.tile([P, GT], F32, name="rstd")
+            nc.vector.reciprocal(out=rstd[:], in_=sd[:])
+            z = zpool.tile([P, GT, PACK, P], F32, name="z")
             for j in range(GT):
                 nc.gpsimd.tensor_scalar(
-                    out=z[:, j, :],
-                    in0=xt[g][:, j, :],
+                    out=z[:, j, :, :],
+                    in0=xt[g][:, j, :].rearrange("p (q t) -> p t q", t=PACK),
                     scalar1=negmu[:, j : j + 1],
                     scalar2=rstd[:, j : j + 1],
                     op0=ALU.add,
@@ -155,7 +155,7 @@ def tile_transformerlayer_pa_t_kernel(
             for t in range(PACK):
                 bank = psum.tile([P, GTOK], F32, name="trb", tag="tr%d" % ((PACK * g + t) % TRB))
                 for j in range(GT):
-                    nc.tensor.transpose(bank[:, j * P : (j + 1) * P], z[:, j, t::PACK], ident[:])
+                    nc.tensor.transpose(bank[:, j * P : (j + 1) * P], z[:, j, t, :], ident[:])
                 banks.append(bank)
             S[("tr", g)] = banks
 
@@ -225,19 +225,20 @@ def tile_transformerlayer_pa_t_kernel(
                 nc.sync.dma_start(out=outs[pr][g], in_=o[:])
 
         for n in range(-4, NG + 3):
+            if 0 <= n + 3 < NG:
+                deviation(n + 3)
             if 0 <= n < NG:
                 affine(n)
             if 0 <= n + 1 < NG:
                 transposes(n + 1)
-            if 0 <= n + 3 < NG:
-                rstd_of(n + 3)
-                normalise(n + 3)
             if 0 <= n - 3 < NG:
                 finish(n - 3)
             if 0 <= n - 1 < NG:
                 regroup(n - 1)
             if 0 <= n - 2 < NG:
                 quantise(n - 2)
+            if 0 <= n + 3 < NG:
+                normalise(n + 3)
             if n + 4 < NG:
                 stats(n + 4)
             if n == -4:

@@ -57,7 +57,7 @@ def tile_transformerlayer_pa_t_kernel(
         sraw = const.tile([P, PACK], BF16, name="sraw")
         braw = const.tile([P, PACK], BF16, name="braw")
         brow = const.tile([P, NPROJ * E], BF16, name="brow")
-        nc.vector.memset(brow[:], 0.0)
+        nc.gpsimd.memset(brow[:], 0.0)
 
         for j in range(GT):
             nc.sync.dma_start(out=xt[0][:, j, :], in_=xg[0][:, j * D : (j + 1) * D])
@@ -224,24 +224,25 @@ def tile_transformerlayer_pa_t_kernel(
                 )
                 nc.sync.dma_start(out=outs[pr][g], in_=o[:])
 
-        for n in range(-4, NG + 3):
-            if 0 <= n + 3 < NG:
-                deviation(n + 3)
+        for n in range(-5, NG + 3):
+            gn = n + 4 if n < -1 else (n + 3 if n > -1 else NG)
+            if 0 <= gn < NG:
+                deviation(gn)
             if 0 <= n < NG:
                 affine(n)
             if 0 <= n + 1 < NG:
                 transposes(n + 1)
-            if 0 <= n - 3 < NG:
-                finish(n - 3)
             if 0 <= n - 1 < NG:
                 regroup(n - 1)
             if 0 <= n - 2 < NG:
                 quantise(n - 2)
-            if 0 <= n + 3 < NG:
-                normalise(n + 3)
-            if n + 4 < NG:
-                stats(n + 4)
-            if n == -4:
+            if 0 <= gn < NG:
+                normalise(gn)
+            if n + 5 < NG:
+                stats(n + 5)
+            if 0 <= n - 3 < NG:
+                finish(n - 3)
+            if n == -5:
                 setup_gain()
             if n == -2:
                 setup_group_weights()

@@ -114,6 +114,8 @@ def tile_transformerlayer_pa_t_kernel(
             nc.tensor.matmul(ps[:, 0 : NPROJ * E], lhsT=ones[:], rhs=brow[:], start=True, stop=True)
             nc.vector.tensor_copy(out=bias[:], in_=ps[:, 0 : NPROJ * E])
 
+        warm = psum.tile([P, GTOK], F32, name="warm")
+
         S = {}
 
         def stats(g):
@@ -156,6 +158,7 @@ def tile_transformerlayer_pa_t_kernel(
                 bank = psum.tile([P, GTOK], F32, name="trb", tag="tr%d" % ((PACK * g + t) % TRB))
                 for j in range(GT):
                     nc.tensor.transpose(bank[:, j * P : (j + 1) * P], z[:, j, t, :], ident[:])
+                nc.tensor.matmul(warm[:, t * P : (t + 1) * P], lhsT=ident[:], rhs=ident[:], start=True, stop=True)
                 banks.append(bank)
             S[("tr", g)] = banks
 

@@ -77,6 +77,8 @@ def tile_transformerlayer_pa_t_kernel(
 
         ident = const.tile([P, P], F32, name="ident")
         make_identity(nc, ident[:])
+        wide = const.tile([P, 2 * P], F32, name="wide")
+        nc.gpsimd.memset(wide[:], 0.0)
         eps_t = const.tile([P, 1], F32, name="eps_t")
         zero_t = const.tile([P, 1], F32, name="zero_t")
         nc.gpsimd.memset(zero_t[:], 0.0)
@@ -158,7 +160,9 @@ def tile_transformerlayer_pa_t_kernel(
                 bank = psum.tile([P, GTOK], F32, name="trb", tag="tr%d" % ((PACK * g + t) % TRB))
                 for j in range(GT):
                     nc.tensor.transpose(bank[:, j * P : (j + 1) * P], z[:, j, t, :], ident[:])
-                nc.tensor.matmul(warm[:, t * P : (t + 1) * P], lhsT=ident[:], rhs=ident[:], start=True, stop=True)
+                if t % 2 == 1:
+                    half = slice(t // 2 * 2 * P, (t // 2 + 1) * 2 * P)
+                    nc.tensor.matmul(warm[:, half], lhsT=ident[:], rhs=wide[:], start=True, stop=True)
                 banks.append(bank)
             S[("tr", g)] = banks
 

@@ -45,6 +45,7 @@ def tile_transformerlayer_pa_t_kernel(
         zpool = ctx.enter_context(tc.tile_pool(name="zpool", bufs=4))
         hpool = ctx.enter_context(tc.tile_pool(name="hpool", bufs=3))
         qpool = ctx.enter_context(tc.tile_pool(name="qpool", bufs=3))
+        jpool = ctx.enter_context(tc.tile_pool(name="jpool", bufs=4))
         opool = ctx.enter_context(tc.tile_pool(name="opool", bufs=4))
         psum = ctx.enter_context(tc.psum_pool(name="psum", bufs=1))
         ctx.enter_context(tc.manual_schedule())
@@ -53,7 +54,10 @@ def tile_transformerlayer_pa_t_kernel(
         for g in range(NG):
             x_t = xpool.tile([P, GT, D], BF16, name="x_t")
             xt.append(x_t)
-        wraw = const.tile([P, PACK, NPROJ * E], BF16, name="wraw")
+        wraw = []
+        for pr in range(NPROJ):
+            w_t = const.tile([P, PACK, E], BF16, name="wraw%d" % pr)
+            wraw.append(w_t)
         sraw = const.tile([P, PACK], BF16, name="sraw")
         braw = const.tile([P, PACK], BF16, name="braw")
         brow = const.tile([P, NPROJ * E], BF16, name="brow")
@@ -63,30 +67,32 @@ def tile_transformerlayer_pa_t_kernel(
             nc.sync.dma_start(out=xt[0][:, j, :], in_=xg[0][:, j * D : (j + 1) * D])
         nc.sync.dma_start(out=sraw[:], in_=ln1_s.rearrange("(p t) -> p t", t=PACK))
         nc.sync.dma_start(out=braw[:], in_=ln1_b.rearrange("(p t) -> p t", t=PACK))
-        for g in (1, 2):
+        for g in (1, 2, 3):
             nc.sync.dma_start(out=xt[g][:].rearrange("p j d -> p (j d)"), in_=xg[g])
-        nc.sync.dma_start(out=wraw[:, :, 0:E], in_=wq_k.rearrange("(p t) h e -> p t (h e)", t=PACK))
-        nc.sync.dma_start(out=wraw[:, :, E : 2 * E], in_=wk_k.rearrange("(p t) e -> p t e", t=PACK))
-        nc.sync.dma_start(out=wraw[:, :, 2 * E : 3 * E], in_=wv_k.rearrange("(p t) e -> p t e", t=PACK))
-        nc.sync.dma_start(out=xt[3][:].rearrange("p j d -> p (j d)"), in_=xg[3])
         nc.sync.dma_start(out=brow[0:1, 0:E], in_=wq_b)
         nc.sync.dma_start(out=brow[0:1, E : 2 * E], in_=wk_b.unsqueeze(0))
         nc.sync.dma_start(out=brow[0:1, 2 * E : 3 * E], in_=wv_b.unsqueeze(0))
-        for g in range(4, NG):
+        nc.sync.dma_start(out=wraw[0][:], in_=wq_k.rearrange("(p t) h e -> p t (h e)", t=PACK))
+        nc.sync.dma_start(out=wraw[1][:], in_=wk_k.rearrange("(p t) e -> p t e", t=PACK))
+        nc.sync.dma_start(out=wraw[2][:], in_=wv_k.rearrange("(p t) e -> p t e", t=PACK))
+        nc.sync.dma_start(out=xt[4][:].rearrange("p j d -> p (j d)"), in_=xg[4])
+        for g in range(5, NG):
             nc.sync.dma_start(out=xt[g][:].rearrange("p j d -> p (j d)"), in_=xg[g])
 
-        ident = const.tile([P, P], F32, name="ident")
-        make_identity(nc, ident[:])
-        wide = const.tile([P, 2 * P], F32, name="wide")
-        nc.gpsimd.memset(wide[:], 0.0)
         eps_t = const.tile([P, 1], F32, name="eps_t")
         zero_t = const.tile([P, 1], F32, name="zero_t")
         nc.gpsimd.memset(zero_t[:], 0.0)
         nc.gpsimd.tensor_scalar(
             out=eps_t[:], in0=zero_t[:], scalar1=EPS, scalar2=1.0, op0=ALU.add, op1=ALU.mult
         )
+        sd_warm = const.tile([P, 1], F32, name="sd_warm")
+        nc.scalar.activation(out=sd_warm[:], in_=zero_t[:], func=ACT.Sqrt, bias=zero_t[:, 0:1], scale=1.0)
         ones = const.tile([P, P], BF16, name="ones")
         nc.gpsimd.memset(ones[:], 1.0)
+        ident = const.tile([P, P], F32, name="ident")
+        make_identity(nc, ident[:])
+        wide = const.tile([P, 2 * P], F32, name="wide")
+        nc.gpsimd.memset(wide[:], 0.0)
 
         scol = const.tile([P, PACK], F32, name="scol")
         bcol = const.tile([P, PACK], F32, name="bcol")
@@ -96,11 +102,14 @@ def tile_transformerlayer_pa_t_kernel(
         wgrp = const.tile([P, NPROJ * E, PACK], BF16, name="wgrp", align_bytes=64)
 
         def setup_gain():
-            nc.vector.tensor_copy(out=scol[:], in_=sraw[:])
-            nc.vector.tensor_copy(out=bcol[:], in_=braw[:])
+            nc.gpsimd.tensor_copy(out=scol[:], in_=sraw[:])
+            nc.gpsimd.tensor_copy(out=bcol[:], in_=braw[:])
 
         def setup_group_weights():
-            nc.scalar.copy(out=wgrp[:], in_=wraw[:].rearrange("p t n -> p n t"))
+            for pr in range(NPROJ):
+                dst = wgrp[:, pr * E : (pr + 1) * E, :]
+                src = wraw[pr][:].rearrange("p t n -> p n t")
+                nc.scalar.copy(out=dst, in_=src)
 
         def setup_quantise_weights():
             for pr in range(NPROJ):
@@ -114,20 +123,56 @@ def tile_transformerlayer_pa_t_kernel(
         def setup_bias():
             ps = psum.tile([P, GT * E], F32, name="ps_bias", tag="mm0")
             nc.tensor.matmul(ps[:, 0 : NPROJ * E], lhsT=ones[:], rhs=brow[:], start=True, stop=True)
-            nc.vector.tensor_copy(out=bias[:], in_=ps[:, 0 : NPROJ * E])
+            S["bias"] = ps
+
+        def copy_bias():
+            ps = S["bias"]
+            nc.scalar.copy(out=bias[:], in_=ps[:, 0 : NPROJ * E])
 
         warm = psum.tile([P, GTOK], F32, name="warm")
 
         S = {}
 
-        def stats(g):
-            st = small.tile([P, GT, 6], F32, name="st")
-            mv = small.tile([P, GT, 2], F32, name="mv")
-            for j in range(GT):
+        def stats(g, tiles=range(GT)):
+            if 0 in tiles:
+                st_t = small.tile([P, GT, 6], F32, name="st")
+                S[("st", g)] = st_t
+            st = S[("st", g)]
+            for j in tiles:
                 nc.vector.bn_stats(out=st[:, j, :], in_=xt[g][:, j, :])
+            if GT - 1 in tiles:
+                mv = small.tile([P, GT, 2], F32, name="mv")
+                for j in range(GT):
+                    nc.vector.bn_aggr(out=mv[:, j, :], in_=st[:, j, :])
+                S[("mv", g)] = mv
+
+        def scalar_sums(g, tiles):
+            if 0 in tiles:
+                sums_t = small.tile([P, GT], F32, name="sums")
+                S[("sum", g)] = sums_t
+            for j in tiles:
+                junk = jpool.tile([P, D], BF16, name="junk")
+                nc.scalar.activation(
+                    out=junk[:], in_=xt[g][:, j, :], func=ACT.Copy, accum_out=S[("sum", g)][:, j : j + 1]
+                )
+
+        def scalar_squares(g):
+            negmu = small.tile([P, GT], F32, name="negmu")
+            nc.scalar.activation(out=negmu[:], in_=S[("sum", g)][:], func=ACT.Copy, scale=-1.0 / D)
+            ssq = small.tile([P, GT], F32, name="ssq")
             for j in range(GT):
-                nc.vector.bn_aggr(out=mv[:, j, :], in_=st[:, j, :])
-            S[("mv", g)] = mv
+                junk = jpool.tile([P, D], BF16, name="junk")
+                nc.scalar.activation(
+                    out=junk[:],
+                    in_=xt[g][:, j, :],
+                    func=ACT.Square,
+                    bias=negmu[:, j : j + 1],
+                    scale=1.0,
+                    accum_out=ssq[:, j : j + 1],
+                )
+            sd = small.tile([P, GT], F32, name="sd")
+            nc.scalar.activation(out=sd[:], in_=ssq[:], func=ACT.Sqrt, bias=eps_t[:, 0:1], scale=1.0 / D)
+            S[("rs", g)] = (negmu, sd)
 
         def deviation(g):
             mv = S[("mv", g)]
@@ -137,10 +182,14 @@ def tile_transformerlayer_pa_t_kernel(
             nc.scalar.activation(out=sd[:], in_=mv[:, :, 1], func=ACT.Sqrt, bias=eps_t[:, 0:1], scale=1.0)
             S[("rs", g)] = (negmu, sd)
 
+        def reciprocal(g):
+            rstd = small.tile([P, GT], F32, name="rstd")
+            nc.vector.reciprocal(out=rstd[:], in_=S[("rs", g)][1][:])
+            S[("rstd", g)] = rstd
+
         def normalise(g):
             negmu, sd = S[("rs", g)]
-            rstd = small.tile([P, GT], F32, name="rstd")
-            nc.vector.reciprocal(out=rstd[:], in_=sd[:])
+            rstd = S[("rstd", g)]
             z = zpool.tile([P, GT, PACK, P], F32, name="z")
             for j in range(GT):
                 nc.gpsimd.tensor_scalar(
@@ -231,30 +280,50 @@ def tile_transformerlayer_pa_t_kernel(
                 )
                 nc.sync.dma_start(out=outs[pr][g], in_=o[:])
 
-        for n in range(-5, NG + 3):
-            gn = n + 4 if n < -1 else (n + 3 if n > -1 else NG)
-            if 0 <= gn < NG:
+        setup_gain()
+        stats(0)
+        scalar_sums(1, (0, 1))
+        deviation(0)
+        scalar_sums(1, (2, 3))
+        stats(2, (0,))
+        reciprocal(0)
+        normalise(0)
+        stats(2, (1, 2, 3))
+        scalar_squares(1)
+        setup_bias()
+        setup_group_weights()
+        copy_bias()
+        transposes(0)
+        stats(3, (0, 1))
+        reciprocal(1)
+        normalise(1)
+        stats(3, (2, 3))
+        deviation(2)
+        stats(4, (0, 1))
+        reciprocal(2)
+        normalise(2)
+        setup_quantise_weights()
+        stats(4, (2, 3))
+        for n in range(0, NG + 3):
+            gn = n + 3
+            if 0 < n and gn < NG:
                 deviation(gn)
-            if 0 <= n < NG:
+            if n < NG:
                 affine(n)
-            if 0 <= n + 1 < NG:
+            if n == 0:
+                deviation(gn)
+            if n + 1 < NG:
                 transposes(n + 1)
             if 0 <= n - 1 < NG:
                 regroup(n - 1)
             if 0 <= n - 2 < NG:
                 quantise(n - 2)
-            if 0 <= gn < NG:
+            if gn < NG:
+                reciprocal(gn)
                 normalise(gn)
             if n + 5 < NG:
                 stats(n + 5)
             if 0 <= n - 3 < NG:
                 finish(n - 3)
-            if n == -5:
-                setup_gain()
-            if n == -2:
-                setup_group_weights()
-            if n == -1:
-                setup_quantise_weights()
-                setup_bias()
             if 0 <= n - 2 < NG:
                 project(n - 2)

from contextlib import ExitStack

import concourse.mybir as mybir
from concourse.masks import make_identity

F32 = mybir.dt.float32
BF16 = mybir.dt.bfloat16
U32 = mybir.dt.uint32
U8 = mybir.dt.uint8
FP8X4 = mybir.dt.float8_e4m3fn_x4
ALU = mybir.AluOpType
ACT = mybir.ActivationFunctionType

P = 128
D = 512
PACK = 4
E = 128
NPROJ = 3
TOKENS = 4 * 2048
GT = 4
GTOK = GT * P
NG = TOKENS // GTOK
EPS = 1e-05
TRB = 4
V_REGROUP = (12, 14)

FLOPS = 2 * TOKENS * D * NPROJ * E


def tile_transformerlayer_pa_t_kernel(
    tc, x, ln1_s, ln1_b, wq_k, wq_b, wk_k, wk_b, wv_k, wv_b, out_0, out_1, out_2
):
    nc = tc.nc
    xg = x.rearrange("b s d -> (b s) d").rearrange("(g p j) d -> g p (j d)", p=P, j=GT)
    outs = [
        out_0.rearrange("b s h e -> (b s h) e").rearrange("(g p j) e -> g p (j e)", p=P, j=GT),
        out_1.rearrange("b s e -> (b s) e").rearrange("(g p j) e -> g p (j e)", p=P, j=GT),
        out_2.rearrange("b s e -> (b s) e").rearrange("(g p j) e -> g p (j e)", p=P, j=GT),
    ]

    with ExitStack() as ctx:
        const = ctx.enter_context(tc.tile_pool(name="const", bufs=1))
        xpool = ctx.enter_context(tc.tile_pool(name="xpool", bufs=NG))
        small = ctx.enter_context(tc.tile_pool(name="small", bufs=8))
        zpool = ctx.enter_context(tc.tile_pool(name="zpool", bufs=4))
        hpool = ctx.enter_context(tc.tile_pool(name="hpool", bufs=3))
        qpool = ctx.enter_context(tc.tile_pool(name="qpool", bufs=3))
        jpool = ctx.enter_context(tc.tile_pool(name="jpool", bufs=4))
        opool = ctx.enter_context(tc.tile_pool(name="opool", bufs=4))
        psum = ctx.enter_context(tc.psum_pool(name="psum", bufs=1))
        ctx.enter_context(tc.manual_schedule())

        xt = []
        for g in range(NG):
            x_t = xpool.tile([P, GT, D], BF16, name="x_t")
            xt.append(x_t)
        wraw = []
        for pr in range(NPROJ):
            w_t = const.tile([P, PACK, E], BF16, name="wraw%d" % pr)
            wraw.append(w_t)
        sraw = const.tile([P, PACK], BF16, name="sraw")
        braw = const.tile([P, PACK], BF16, name="braw")
        brow = const.tile([P, NPROJ * E], BF16, name="brow")
        nc.gpsimd.memset(brow[:], 0.0)

        for j in range(GT):
            nc.sync.dma_start(out=xt[0][:, j, :], in_=xg[0][:, j * D : (j + 1) * D])
        nc.sync.dma_start(out=sraw[:], in_=ln1_s.rearrange("(p t) -> p t", t=PACK))
        nc.sync.dma_start(out=braw[:], in_=ln1_b.rearrange("(p t) -> p t", t=PACK))
        for g in (1, 2, 3):
            nc.sync.dma_start(out=xt[g][:].rearrange("p j d -> p (j d)"), in_=xg[g])
        nc.sync.dma_start(out=brow[0:1, 0:E], in_=wq_b)
        nc.sync.dma_start(out=brow[0:1, E : 2 * E], in_=wk_b.unsqueeze(0))
        nc.sync.dma_start(out=brow[0:1, 2 * E : 3 * E], in_=wv_b.unsqueeze(0))
        nc.sync.dma_start(out=wraw[0][:], in_=wq_k.rearrange("(p t) h e -> p t (h e)", t=PACK))
        nc.sync.dma_start(out=wraw[1][:], in_=wk_k.rearrange("(p t) e -> p t e", t=PACK))
        nc.sync.dma_start(out=wraw[2][:], in_=wv_k.rearrange("(p t) e -> p t e", t=PACK))
        nc.sync.dma_start(out=xt[4][:].rearrange("p j d -> p (j d)"), in_=xg[4])
        for g in range(5, NG):
            nc.sync.dma_start(out=xt[g][:].rearrange("p j d -> p (j d)"), in_=xg[g])

        eps_t = const.tile([P, 1], F32, name="eps_t")
        zero_t = const.tile([P, 1], F32, name="zero_t")
        nc.gpsimd.memset(zero_t[:], 0.0)
        nc.gpsimd.tensor_scalar(
            out=eps_t[:], in0=zero_t[:], scalar1=EPS, scalar2=1.0, op0=ALU.add, op1=ALU.mult
        )
        sd_warm = const.tile([P, 1], F32, name="sd_warm")
        nc.scalar.activation(out=sd_warm[:], in_=zero_t[:], func=ACT.Sqrt, bias=zero_t[:, 0:1], scale=1.0)
        ones = const.tile([P, P], BF16, name="ones")
        nc.gpsimd.memset(ones[:], 1.0)
        ident = const.tile([P, P], F32, name="ident")
        make_identity(nc, ident[:])
        wide = const.tile([P, 2 * P], F32, name="wide")
        nc.gpsimd.memset(wide[:], 0.0)

        scol = const.tile([P, PACK], F32, name="scol")
        bcol = const.tile([P, PACK], F32, name="bcol")
        bias = const.tile([P, NPROJ * E], BF16, name="bias")
        wcodes = const.tile([P, NPROJ * E], U32, name="wcodes", align_bytes=64)
        wscl = const.tile([P, NPROJ * E], U8, name="wscl", align_bytes=64)
        wgrp = const.tile([P, NPROJ * E, PACK], BF16, name="wgrp", align_bytes=64)

        def setup_gain():
            nc.gpsimd.tensor_copy(out=scol[:], in_=sraw[:])
            nc.gpsimd.tensor_copy(out=bcol[:], in_=braw[:])

        def setup_group_weights():
            for pr in range(NPROJ):
                dst = wgrp[:, pr * E : (pr + 1) * E, :]
                src = wraw[pr][:].rearrange("p t n -> p n t")
                nc.scalar.copy(out=dst, in_=src)

        def setup_quantise_weights():
            for pr in range(NPROJ):
                cols = slice(pr * E, (pr + 1) * E)
                nc.vector.quantize_mx(
                    out=wcodes[:, cols].bitcast(FP8X4),
                    scales=wscl[:, cols],
                    in_=wgrp[:, cols, :].rearrange("p n t -> p (n t)"),
                )

        def setup_bias():
            ps = psum.tile([P, GT * E], F32, name="ps_bias", tag="mm0")
            nc.tensor.matmul(ps[:, 0 : NPROJ * E], lhsT=ones[:], rhs=brow[:], start=True, stop=True)
            S["bias"] = ps

        def copy_bias():
            ps = S["bias"]
            nc.scalar.copy(out=bias[:], in_=ps[:, 0 : NPROJ * E])

        warm = psum.tile([P, GTOK], F32, name="warm")

        S = {}

        def stats(g, tiles=range(GT)):
            if 0 in tiles:
                st_t = small.tile([P, GT, 6], F32, name="st")
                S[("st", g)] = st_t
            st = S[("st", g)]
            for j in tiles:
                nc.vector.bn_stats(out=st[:, j, :], in_=xt[g][:, j, :])
            if GT - 1 in tiles:
                mv = small.tile([P, GT, 2], F32, name="mv")
                for j in range(GT):
                    nc.vector.bn_aggr(out=mv[:, j, :], in_=st[:, j, :])
                S[("mv", g)] = mv

        def scalar_sums(g, tiles):
            if 0 in tiles:
                sums_t = small.tile([P, GT], F32, name="sums")
                S[("sum", g)] = sums_t
            for j in tiles:
                junk = jpool.tile([P, D], BF16, name="junk")
                nc.scalar.activation(
                    out=junk[:], in_=xt[g][:, j, :], func=ACT.Copy, accum_out=S[("sum", g)][:, j : j + 1]
                )

        def scalar_squares(g):
            negmu = small.tile([P, GT], F32, name="negmu")
            nc.scalar.activation(out=negmu[:], in_=S[("sum", g)][:], func=ACT.Copy, scale=-1.0 / D)
            ssq = small.tile([P, GT], F32, name="ssq")
            for j in range(GT):
                junk = jpool.tile([P, D], BF16, name="junk")
                nc.scalar.activation(
                    out=junk[:],
                    in_=xt[g][:, j, :],
                    func=ACT.Square,
                    bias=negmu[:, j : j + 1],
                    scale=1.0,
                    accum_out=ssq[:, j : j + 1],
                )
            sd = small.tile([P, GT], F32, name="sd")
            nc.scalar.activation(out=sd[:], in_=ssq[:], func=ACT.Sqrt, bias=eps_t[:, 0:1], scale=1.0 / D)
            S[("rs", g)] = (negmu, sd)

        def deviation(g):
            mv = S[("mv", g)]
            negmu = small.tile([P, GT], F32, name="negmu")
            nc.scalar.activation(out=negmu[:], in_=mv[:, :, 0], func=ACT.Copy, scale=-1.0)
            sd = small.tile([P, GT], F32, name="sd")
            nc.scalar.activation(out=sd[:], in_=mv[:, :, 1], func=ACT.Sqrt, bias=eps_t[:, 0:1], scale=1.0)
            S[("rs", g)] = (negmu, sd)

        def reciprocal(g):
            rstd = small.tile([P, GT], F32, name="rstd")
            nc.vector.reciprocal(out=rstd[:], in_=S[("rs", g)][1][:])
            S[("rstd", g)] = rstd

        def normalise(g):
            negmu, sd = S[("rs", g)]
            rstd = S[("rstd", g)]
            z = zpool.tile([P, GT, PACK, P], F32, name="z")
            for j in range(GT):
                nc.gpsimd.tensor_scalar(
                    out=z[:, j, :, :],
                    in0=xt[g][:, j, :].rearrange("p (q t) -> p t q", t=PACK),
                    scalar1=negmu[:, j : j + 1],
                    scalar2=rstd[:, j : j + 1],
                    op0=ALU.add,
                    op1=ALU.mult,
                )
            S[("z", g)] = z

        def transposes(g):
            z = S[("z", g)]
            banks = []
            for t in range(PACK):
                bank = psum.tile([P, GTOK], F32, name="trb", tag="tr%d" % ((PACK * g + t) % TRB))
                for j in range(GT):
                    nc.tensor.transpose(bank[:, j * P : (j + 1) * P], z[:, j, t, :], ident[:])
                if t % 2 == 1:
                    half = slice(t // 2 * 2 * P, (t // 2 + 1) * 2 * P)
                    nc.tensor.matmul(warm[:, half], lhsT=ident[:], rhs=wide[:], start=True, stop=True)
                banks.append(bank)
            S[("tr", g)] = banks

        def affine(g):
            banks = S[("tr", g)]
            hT = hpool.tile([P, PACK, GTOK], BF16, name="hT")
            for t in range(PACK):
                nc.scalar.activation(
                    out=hT[:, t, :],
                    in_=banks[t][:],
                    func=ACT.Identity,
                    scale=scol[:, t : t + 1],
                    bias=bcol[:, t : t + 1],
                )
            S[("hT", g)] = hT

        def regroup(g):
            hT = S[("hT", g)]
            hG = hpool.tile([P, GTOK, PACK], BF16, name="hG", align_bytes=64)
            dst = hG[:].rearrange("p (c i) t -> p c t i", i=4)
            src = hT[:].rearrange("p t (c i) -> p c t i", i=4)
            if g in V_REGROUP:
                nc.vector.tensor_copy(out=dst, in_=src)
            else:
                nc.scalar.copy(out=dst, in_=src)
            S[("hG", g)] = hG

        def quantise(g):
            hG = S[("hG", g)]
            codes = qpool.tile([P, GTOK], U32, name="codes", align_bytes=64)
            scl = qpool.tile([P, GTOK], U8, name="scl", align_bytes=64)
            nc.vector.quantize_mx(
                out=codes[:].bitcast(FP8X4), scales=scl[:], in_=hG[:].rearrange("p c t -> p (c t)")
            )
            S[("q", g)] = (codes, scl)

        def project(g):
            codes, scl = S[("q", g)]
            banks = []
            for pr in range(NPROJ):
                bank = psum.tile([P, GT * E], F32, name="mmb", tag="mm%d" % pr)
                wc = slice(pr * E, (pr + 1) * E)
                for j in range(GT):
                    tk = slice(j * P, (j + 1) * P)
                    nc.tensor.matmul_mx(
                        out=bank[:, j * E : (j + 1) * E],
                        lhsT=codes[:, tk].bitcast(FP8X4),
                        lhsT_scale=scl[:, tk],
                        rhs=wcodes[:, wc].bitcast(FP8X4),
                        rhs_scale=wscl[:, wc],
                        start=True,
                        stop=True,
                    )
                banks.append(bank)
            S[("mm", g)] = banks

        def finish(g):
            banks = S[("mm", g)]
            for pr in range(NPROJ):
                o = opool.tile([P, GT * E], F32, name="o%d" % pr)
                nc.vector.tensor_tensor(
                    out=o[:].rearrange("p (j e) -> p j e", e=E),
                    in0=banks[pr][:].rearrange("p (j e) -> p j e", e=E),
                    in1=bias[:, pr * E : (pr + 1) * E].unsqueeze(1).to_broadcast([P, GT, E]),
                    op=ALU.add,
                )
                nc.sync.dma_start(out=outs[pr][g], in_=o[:])

        setup_gain()
        stats(0)
        scalar_sums(1, (0, 1))
        deviation(0)
        scalar_sums(1, (2, 3))
        stats(2, (0,))
        reciprocal(0)
        normalise(0)
        stats(2, (1, 2, 3))
        scalar_squares(1)
        setup_bias()
        setup_group_weights()
        copy_bias()
        transposes(0)
        stats(3, (0, 1))
        reciprocal(1)
        normalise(1)
        stats(3, (2, 3))
        deviation(2)
        stats(4, (0, 1))
        reciprocal(2)
        normalise(2)
        setup_quantise_weights()
        stats(4, (2, 3))
        for n in range(0, NG + 3):
            gn = n + 3
            if 0 < n and gn < NG:
                deviation(gn)
            if n < NG:
                affine(n)
            if n == 0:
                deviation(gn)
            if n + 1 < NG:
                transposes(n + 1)
            if 0 <= n - 1 < NG:
                regroup(n - 1)
            if 0 <= n - 2 < NG:
                quantise(n - 2)
            if gn < NG:
                reciprocal(gn)
                normalise(gn)
            if n + 5 < NG:
                stats(n + 5)
            if 0 <= n - 3 < NG:
                finish(n - 3)
            if 0 <= n - 2 < NG:
                project(n - 2)
